import numpy as np
import ml_dtypes


def mxq(x, axis, fmt="e4m3"):
    dtype, down = {"e4m3": (ml_dtypes.float8_e4m3fn, 7), "e5m2": (ml_dtypes.float8_e5m2, 14)}[fmt]
    v = np.moveaxis(np.asarray(x, np.float32).astype(ml_dtypes.bfloat16).astype(np.float64), axis, -1)
    blocks = v.reshape(v.shape[:-1] + (-1, 32))
    amax = np.abs(blocks).max(-1, keepdims=True)
    byte = np.maximum(np.where(amax > 0, np.frexp(amax)[1] - 1 + 127, 0) - down, 1)
    scale = np.exp2(byte - 127.0)
    codes = (blocks / scale).astype(np.float32).astype(dtype).astype(np.float64)
    return np.moveaxis((codes * scale).reshape(v.shape), -1, axis)


WIDE = False


def mx_kscale(k):
    if not WIDE:
        return np.ones(k)
    levels = np.array([10, -10, 5, -5, 0])
    a = np.random.permutation(np.resize(levels, k // 512 * 4)).reshape(k // 512, 4)
    idx = np.arange(k)
    return np.exp2(a[idx // 512, idx % 128 // 32])


BF16 = ml_dtypes.bfloat16


def bf(x):
    return np.asarray(x, np.float32).astype(BF16)


def f64(x):
    return np.asarray(x).astype(np.float64)


E2M1 = np.array([0.0, 0.5, 1.0, 1.5, 2.0, 3.0, 4.0, 6.0, -0.0, -0.5, -1.0, -1.5, -2.0, -3.0, -4.0, -6.0])


def pack_weight(w, fmt):
    k, n = w.shape
    w = f64(bf(w)).reshape(k // 32, 32, n)
    amax = np.abs(w).max(1)
    if fmt == "e4m3":
        byte = np.frexp(amax)[1] - 1 + 127 - 7
    else:
        mant, ex = np.frexp(amax / 6.0)
        byte = np.where(mant > 0.5, ex, ex - 1) + 127
    byte = np.clip(np.where(amax > 0, byte, 1), 1, 254)
    scaled = (w * np.exp2(127.0 - byte)[:, None, :]).reshape(k, n).astype(np.float32)
    by_word = np.ascontiguousarray(scaled.reshape(k // 512, 128, 4, n).transpose(0, 1, 3, 2))
    if fmt == "e4m3":
        words = by_word.astype(ml_dtypes.float8_e4m3fn).view(np.uint8)
    else:
        c = by_word.astype(ml_dtypes.float4_e2m1fn).view(np.uint8) & 0xF
        words = c[..., 0::2] | (c[..., 1::2] << 4)
    return np.ascontiguousarray(words), np.ascontiguousarray(byte.astype(np.uint8).reshape(k // 512, 16, n))


def unpack_weight(words, scales, fmt):
    g, p, n, _ = words.shape
    if fmt == "e4m3":
        vals = np.ascontiguousarray(words).view(ml_dtypes.float8_e4m3fn).astype(np.float64)
    else:
        nib = np.empty((g, p, n, 4), np.uint8)
        nib[..., 0::2] = words & 0xF
        nib[..., 1::2] = words >> 4
        vals = E2M1[nib]
    vals = vals * np.repeat(np.exp2(scales.astype(np.float64) - 127.0), 8, axis=1)[..., None]
    return vals.transpose(0, 1, 3, 2).reshape(g * 512, n)


B, C, P, NH, NW = 2, 8, 16, 8, 8
D = C * P * P
QK_SCALE = 1.0
FMT = "e4m3"


def rel_bias(p):
    i = np.arange(p, dtype=np.float64)
    down = np.exp(-i / (p / 2))[:, None] * np.ones((1, p))
    right = down.T
    br = np.exp(-(i[:, None] + i[None, :]) / (p / 2))
    return np.stack([
        np.rot90(br, 2), np.flip(down, 0), np.rot90(br, 1),
        np.flip(right, 1), np.ones((p, p)), right,
        np.rot90(br, 3), down, br,
    ], axis=0)


def setup_inputs():
    s = mx_kscale(D)
    sx = np.tile(s.reshape(C, P, P), (1, NH, NW))
    x = bf(np.random.standard_normal((B, C, NH * P, NW * P)) * sx)
    w = np.random.standard_normal((3 * D, D)) / np.sqrt(D) / s
    words, scales = pack_weight(np.ascontiguousarray(w.T), FMT)
    b_qkv = bf(np.random.standard_normal(3 * D) * 0.5)
    return {"x": x,
            "W_qkv_words": words,
            "W_qkv_scales": scales,
            "b_qkv": b_qkv}


def reference(x, W_qkv_words, W_qkv_scales, b_qkv):
    p, c = P, C
    b, _, h, w = x.shape
    nh, nw = h // p, w // p
    feat = f64(x).reshape(b, c, nh, p, nw, p).transpose(0, 2, 4, 1, 3, 5).reshape(b, nh, nw, c * p * p)
    y = mxq(feat, 3, "e4m3") @ unpack_weight(W_qkv_words, W_qkv_scales, FMT)
    qkv = np.pad(y, ((0, 0), (1, 1), (1, 1), (0, 0))) + f64(b_qkv)
    qkv = qkv.reshape(b, nh + 2, nw + 2, 3, c, p, p)
    core_q = qkv[:, 1:nh + 1, 1:nw + 1, 0] * QK_SCALE
    k = np.stack([qkv[:, di:di + nh, dj:dj + nw, 1] for di in range(3) for dj in range(3)], axis=3)
    v = np.stack([qkv[:, di:di + nh, dj:dj + nw, 2] for di in range(3) for dj in range(3)], axis=3)
    bias = rel_bias(p)
    attn = core_q[:, :, :, None] * k * bias[:, None]
    out = np.sum(attn * v, axis=3)
    return out.transpose(0, 3, 1, 4, 2, 5).reshape(b, c, nh * p, nw * p)

@@ -1,0 +1,256 @@
+from contextlib import ExitStack
+
+import concourse.mybir as mybir
+from concourse.masks import make_identity
+
+F32 = mybir.dt.float32
+BF16 = mybir.dt.bfloat16
+I32 = mybir.dt.int32
+U32 = mybir.dt.uint32
+U8 = mybir.dt.uint8
+FP8X4 = mybir.dt.float8_e4m3fn_x4
+ALU = mybir.AluOpType
+ACT = mybir.ActivationFunctionType
+
+P = 128
+FLOPS = 2 * 128 * 2048 * 6144
+
+
+def tile_attentionconv_w_kernel(tc, x, W_qkv_words, W_qkv_scales, b_qkv, out):
+    nc = tc.nc
+    with ExitStack() as ctx:
+        const = ctx.enter_context(tc.tile_pool(name="const", bufs=1))
+        wpool = ctx.enter_context(tc.tile_pool(name="wpool", bufs=1))
+        work = ctx.enter_context(tc.tile_pool(name="work", bufs=3))
+        ps_t = ctx.enter_context(tc.psum_pool(name="ps_t", bufs=3))
+        ps_m = ctx.enter_context(tc.psum_pool(name="ps_m", bufs=5))
+
+        xh = const.tile([P, 16, 128], BF16, name="xh")
+        nc.sync.dma_start(out=xh[:], in_=x.rearrange("b c h w -> h (b c) w"))
+
+        bb = const.tile([48, 128], BF16, name="bb")
+        nc.scalar.dma_start(out=bb[:], in_=b_qkv.rearrange("(m p) -> m p", p=128))
+
+        planes = const.tile([P, 6144], U8, name="planes", align_bytes=64)
+        nc.vector.memset(planes[:].bitcast(I32), 0)
+        for quad in range(4):
+            nc.sync.dma_start(
+                out=planes[32 * quad : 32 * quad + 16, :].bitcast(I32),
+                in_=W_qkv_scales[:, 4 * quad : 4 * quad + 4, :].bitcast(I32),
+            )
+
+        w_view = W_qkv_words.rearrange("g p n t -> p g (n t)")
+        slab_order = []
+        for s in range(4):
+            slab_order.append((1, s))
+            slab_order.append((2, s))
+        for s in range(4):
+            slab_order.append((0, s))
+        w_tiles = {}
+        for third, s in slab_order:
+            wt = wpool.tile([P, 4, 512], U32, name="w%d_%d" % (third, s), align_bytes=64)
+            n0 = third * 2048 + s * 512
+            nc.sync.dma_start(
+                out=wt[:].bitcast(I32),
+                in_=w_view[:, :, 4 * n0 : 4 * (n0 + 512)].bitcast(I32),
+            )
+            w_tiles[(third, s)] = wt
+
+        ident = const.tile([P, P], F32, name="ident")
+        make_identity(nc, ident[:])
+
+        pidx = const.tile([P, 1], I32, name="pidx")
+        nc.gpsimd.iota(pidx[:], pattern=[[1, 1]], base=0, channel_multiplier=1)
+
+        xw = xh[:].bitcast(F32).rearrange(
+            "p (bg chl) (j sq u) -> p chl sq bg j u", chl=2, sq=4, u=2
+        )
+        p1 = const.tile([P, 8, 128], F32, name="p1")
+        nc.vector.tensor_copy(
+            out=p1[:, 0:4, :].rearrange("p sq (bg j u) -> p sq bg j u", j=8, u=2),
+            in_=xw[:, 0],
+        )
+        for sq in range(4):
+            nc.scalar.copy(
+                out=p1[:, 4 + sq, :].rearrange("p (bg j u) -> p bg j u", j=8, u=2),
+                in_=xw[:, 1, sq],
+            )
+        s1 = const.tile([P, 8, 128], F32, name="s1")
+        s1v = s1[:].rearrange("p i (chl r sq) -> p chl i r sq", chl=2, sq=4)
+        for chl in range(2):
+            ps1 = ps_t.tile([P, 512], F32, name="ps1", tag="tp")
+            for sq in range(4):
+                nc.tensor.transpose(
+                    out=ps1[:, sq * 128 : (sq + 1) * 128], in_=p1[:, chl * 4 + sq, :], identity=ident[:]
+                )
+            src = ps1[:].rearrange("p (sq i r) -> p i r sq", sq=4, i=8)
+            if chl == 0:
+                nc.vector.tensor_copy(out=s1v[:, chl], in_=src)
+            else:
+                nc.scalar.copy(out=s1v[:, chl], in_=src)
+
+        fin = const.tile([P, 2048], BF16, name="fin", align_bytes=64)
+        finw = fin[:].bitcast(F32).rearrange("p (gj b i u) -> p b gj i u", gj=32, b=2, i=8, u=2)
+        for h in range(2):
+            ps2 = ps_t.tile([P, 512], F32, name="ps2", tag="tp")
+            for ii in range(4):
+                nc.tensor.transpose(
+                    out=ps2[:, ii * 128 : (ii + 1) * 128], in_=s1[:, 4 * h + ii, :], identity=ident[:]
+                )
+            src = ps2[:].rearrange("p (i b gj u) -> p b gj i u", i=4, b=2, gj=32, u=2)
+            for b in range(2):
+                dst = finw[:, b, :, 4 * h : 4 * h + 4, :]
+                if h == 0:
+                    nc.vector.tensor_copy(out=dst, in_=src[:, b])
+                else:
+                    nc.scalar.copy(out=dst, in_=src[:, b])
+
+        fcodes = const.tile([P, 512], U32, name="fcodes", align_bytes=64)
+        fsc = const.tile([P, 512], U8, name="fsc", align_bytes=64)
+        nc.vector.quantize_mx(out=fcodes[:].bitcast(FP8X4), scales=fsc[:], in_=fin[:])
+
+        bz = const.tile([P, P], F32, name="bz")
+        nc.vector.memset(bz[:], 0.0)
+        nc.vector.tensor_copy(out=bz[0:48, :], in_=bb[:])
+        psb = ps_t.tile([P, 512], F32, name="psb", tag="tp")
+        nc.tensor.transpose(out=psb[:, 0:128], in_=bz[:], identity=ident[:])
+        bias_t = const.tile([P, 48], F32, name="bias_t")
+        nc.vector.tensor_copy(out=bias_t[:], in_=psb[:, 0:48])
+
+        si = const.tile([P, 2], I32, name="si")
+        nc.vector.tensor_single_scalar(out=si[:, 0:1], in_=pidx[:], scalar=15, op=ALU.bitwise_and)
+        nc.vector.tensor_single_scalar(out=si[:, 1:2], in_=pidx[:], scalar=4, op=ALU.arith_shift_right)
+        sf = const.tile([P, 2], F32, name="sf")
+        nc.vector.tensor_copy(out=sf[:], in_=si[:])
+        arg = const.tile([P, 6], F32, name="arg")
+        specs = [(0, -15.0, 0.125), (0, 0.0, -0.125), (1, -15.0, 0.125), (1, -7.0, 0.125), (1, 0.0, -0.125), (1, 8.0, -0.125)]
+        for col, (which, shift, factor) in enumerate(specs):
+            nc.vector.tensor_scalar(
+                out=arg[:, col : col + 1], in0=sf[:, which : which + 1],
+                scalar1=shift, scalar2=factor, op0=ALU.add, op1=ALU.mult,
+            )
+        tab = const.tile([P, 6], F32, name="tab")
+        nc.scalar.activation(out=tab[:], in_=arg[:], func=ACT.Exp)
+        sar = const.tile([P, 2], F32, name="sar")
+        nc.vector.tensor_tensor(out=sar[:], in0=tab[:, 2:4], in1=tab[:, 4:6], op=ALU.add)
+        nc.vector.tensor_single_scalar(out=sar[:], in_=sar[:], scalar=1.0, op=ALU.add)
+
+        beta = const.tile([P, 2, 8], F32, name="beta")
+        nc.vector.tensor_tensor(
+            out=beta[:],
+            in0=bias_t[:, 16:32].rearrange("p (ch rh) -> p rh ch", rh=2),
+            in1=bias_t[:, 32:48].rearrange("p (ch rh) -> p rh ch", rh=2),
+            op=ALU.mult,
+        )
+        betar = const.tile([P, 2, 8], F32, name="betar")
+        nc.vector.tensor_tensor(
+            out=betar[:], in0=beta[:], in1=sar[:].unsqueeze(2).to_broadcast([P, 2, 8]), op=ALU.mult
+        )
+
+        kv = const.tile([P, 2, 8, 16, 16], F32, name="kv")
+        nc.vector.tensor_copy(
+            out=kv[:, :, :, :, 3:13:9],
+            in_=beta[:].unsqueeze(3).unsqueeze(4).to_broadcast([P, 2, 8, 16, 2]),
+        )
+        tt = const.tile([P, 2, 8, 20, 8], F32, name="tt")
+        nc.vector.tensor_copy(
+            out=tt[:].rearrange("p a c (j q) i -> p a c j (q i)", q=2)[:, :, :, 0:10:9, :],
+            in_=betar[:].unsqueeze(3).unsqueeze(4).to_broadcast([P, 2, 8, 2, 16]),
+        )
+        uu = const.tile([P, 2, 8, 16, 8], F32, name="uu")
+        oo = const.tile([P, 2, 8, 2, 2, 4, 8], F32, name="oo")
+
+        def project(third, s):
+            acc = ps_m.tile([P, 512], F32, name="acc", tag="mm")
+            wt = w_tiles[(third, s)]
+            for slot in range(4):
+                n0 = third * 2048 + s * 512 + slot * 128
+                for g in range(4):
+                    nc.tensor.matmul_mx(
+                        out=acc[:, slot * 128 : (slot + 1) * 128],
+                        lhsT=wt[:, g, slot * 128 : (slot + 1) * 128].bitcast(FP8X4),
+                        lhsT_scale=planes[4 * g : 128, n0 : n0 + 128],
+                        rhs=fcodes[:, g * 128 : (g + 1) * 128].bitcast(FP8X4),
+                        rhs_scale=fsc[:, g * 128 : (g + 1) * 128],
+                        start=(g == 0),
+                        stop=(g == 3),
+                    )
+            return acc
+
+        for s in range(4):
+            acc_k = project(1, s)
+            k1 = work.tile([P, 512], F32, name="k1")
+            for slot in range(4):
+                c = 4 * s + slot
+                nc.scalar.activation(
+                    out=k1[:, slot * 128 : (slot + 1) * 128], in_=acc_k[:, slot * 128 : (slot + 1) * 128],
+                    func=ACT.Identity, bias=bias_t[:, 16 + c : 17 + c], scale=1.0,
+                )
+            acc_v = project(2, s)
+            for slot in range(4):
+                c = 4 * s + slot
+                nc.vector.scalar_tensor_tensor(
+                    out=kv[:, c % 2, c // 2, :, 4:12],
+                    in0=acc_v[:, slot * 128 : (slot + 1) * 128].rearrange("p (a i) -> p a i", i=8),
+                    scalar=bias_t[:, 32 + c : 33 + c],
+                    in1=k1[:, slot * 128 : (slot + 1) * 128].rearrange("p (a i) -> p a i", i=8),
+                    op0=ALU.add, op1=ALU.mult,
+                )
+            ch0 = 2 * s
+            for rh in range(2):
+                kvv = kv[:, rh, ch0 : ch0 + 2]
+                tmp = work.tile([P, 2, 16, 8], F32, name="tmp")
+                nc.vector.scalar_tensor_tensor(
+                    out=tmp[:], in0=kvv[:, :, :, 3:11], scalar=tab[:, 2 + rh : 3 + rh], in1=kvv[:, :, :, 4:12],
+                    op0=ALU.mult, op1=ALU.add,
+                )
+                ttv = tt[:, rh, ch0 : ch0 + 2]
+                nc.vector.scalar_tensor_tensor(
+                    out=ttv[:, :, 2:18, :], in0=kvv[:, :, :, 5:13], scalar=tab[:, 4 + rh : 5 + rh], in1=tmp[:],
+                    op0=ALU.mult, op1=ALU.add,
+                )
+                tmp2 = work.tile([P, 2, 16, 8], F32, name="tmp2")
+                nc.vector.scalar_tensor_tensor(
+                    out=tmp2[:], in0=ttv[:, :, 0:16, :], scalar=tab[:, 0:1], in1=ttv[:, :, 2:18, :],
+                    op0=ALU.mult, op1=ALU.add,
+                )
+                nc.vector.scalar_tensor_tensor(
+                    out=uu[:, rh, ch0 : ch0 + 2], in0=ttv[:, :, 4:20, :], scalar=tab[:, 1:2], in1=tmp2[:],
+                    op0=ALU.mult, op1=ALU.add,
+                )
+
+        for s in range(4):
+            acc_q = project(0, s)
+            for slot in range(4):
+                c = 4 * s + slot
+                ch, rh = c // 2, c % 2
+                nc.vector.scalar_tensor_tensor(
+                    out=oo[:, ch // 4, :, :, rh, ch % 4, :].rearrange("p j b i -> p (j b) i"),
+                    in0=acc_q[:, slot * 128 : (slot + 1) * 128].rearrange("p (a i) -> p a i", i=8),
+                    scalar=bias_t[:, c : c + 1],
+                    in1=uu[:, rh, ch],
+                    op0=ALU.add, op1=ALU.mult,
+                )
+            if s % 2 == 1:
+                cg = s // 2
+                o_rows = work.tile([P, 8, 8, 16], F32, name="o_rows", bufs=2)
+                for hj in range(2):
+                    pso = ps_t.tile([P, 512], F32, name="pso", tag="tp")
+                    for jj in range(4):
+                        nc.tensor.transpose(
+                            out=pso[:, jj * 128 : (jj + 1) * 128],
+                            in_=oo[:, cg, 4 * hj + jj].rearrange("p b rh c i -> p (b rh c i)"),
+                            identity=ident[:],
+                        )
+                    src = pso[:].rearrange("p (j r s) -> p r j s", j=4, r=8)
+                    if hj == 0:
+                        nc.scalar.copy(out=o_rows[:, :, 0:4, :], in_=src)
+                    else:
+                        nc.vector.tensor_copy(out=o_rows[:, :, 4:8, :], in_=src)
+                for b in range(2):
+                    dst = out[b, 4 * cg : 4 * cg + 4].rearrange("c (i rh r) w -> rh (c i) (r w)", rh=2, r=8)
+                    for rh in range(2):
+                        p0 = b * 64 + rh * 32
+                        nc.sync.dma_start(
+                            out=dst[rh], in_=o_rows[p0 : p0 + 32].rearrange("p r j s -> p (r j s)")
+                        )

@@ -40,21 +40,22 @@ def tile_attentionconv_w_kernel(tc, x, W_qkv_words, W_qkv_scales, b_qkv, out):
             )
 
         w_view = W_qkv_words.rearrange("g p n t -> p g (n t)")
-        slab_order = []
-        for s in range(4):
-            slab_order.append((1, s))
-            slab_order.append((2, s))
-        for s in range(4):
-            slab_order.append((0, s))
+        loads = [
+            (1, 0, 1024, 1), (2, 0, 1024, 1), (1, 1024, 1024, 1), (2, 1024, 1024, 1),
+            (0, 0, 1024, 1), (0, 1024, 512, 1), (0, 1536, 512, 4),
+        ]
         w_tiles = {}
-        for third, s in slab_order:
-            wt = wpool.tile([P, 4, 512], U32, name="w%d_%d" % (third, s), align_bytes=64)
-            n0 = third * 2048 + s * 512
-            nc.sync.dma_start(
-                out=wt[:].bitcast(I32),
-                in_=w_view[:, :, 4 * n0 : 4 * (n0 + 512)].bitcast(I32),
-            )
-            w_tiles[(third, s)] = wt
+        for third, c0, cols, pieces in loads:
+            wt = wpool.tile([P, 4, cols], U32, name="w%d_%d" % (third, c0), align_bytes=64)
+            n0 = third * 2048 + c0
+            gs = 4 // pieces
+            for piece in range(pieces):
+                nc.sync.dma_start(
+                    out=wt[:, piece * gs : (piece + 1) * gs, :].bitcast(I32),
+                    in_=w_view[:, piece * gs : (piece + 1) * gs, 4 * n0 : 4 * (n0 + cols)].bitcast(I32),
+                )
+            for s in range(c0 // 512, (c0 + cols) // 512):
+                w_tiles[(third, s)] = (wt, s * 512 - c0)
 
         ident = const.tile([P, P], F32, name="ident")
         make_identity(nc, ident[:])
@@ -160,22 +161,36 @@ def tile_attentionconv_w_kernel(tc, x, W_qkv_words, W_qkv_scales, b_qkv, out):
         uu = const.tile([P, 2, 8, 16, 8], F32, name="uu")
         oo = const.tile([P, 2, 8, 2, 2, 4, 8], F32, name="oo")
 
+        def one_pass(dst, third, s, slot, g):
+            wt, off = w_tiles[(third, s)]
+            lc = off + slot * 128
+            n0 = third * 2048 + s * 512 + slot * 128
+            nc.tensor.matmul_mx(
+                out=dst,
+                lhsT=wt[:, g, lc : lc + 128].bitcast(FP8X4),
+                lhsT_scale=planes[4 * g : 128, n0 : n0 + 128],
+                rhs=fcodes[:, g * 128 : (g + 1) * 128].bitcast(FP8X4),
+                rhs_scale=fsc[:, g * 128 : (g + 1) * 128],
+                start=(g == 0),
+                stop=(g == 3),
+            )
+
         def project(third, s):
             acc = ps_m.tile([P, 512], F32, name="acc", tag="mm")
-            wt = w_tiles[(third, s)]
             for slot in range(4):
-                n0 = third * 2048 + s * 512 + slot * 128
                 for g in range(4):
-                    nc.tensor.matmul_mx(
-                        out=acc[:, slot * 128 : (slot + 1) * 128],
-                        lhsT=wt[:, g, slot * 128 : (slot + 1) * 128].bitcast(FP8X4),
-                        lhsT_scale=planes[4 * g : 128, n0 : n0 + 128],
-                        rhs=fcodes[:, g * 128 : (g + 1) * 128].bitcast(FP8X4),
-                        rhs_scale=fsc[:, g * 128 : (g + 1) * 128],
-                        start=(g == 0),
-                        stop=(g == 3),
-                    )
-            return acc
+                    one_pass(acc[:, slot * 128 : (slot + 1) * 128], third, s, slot, g)
+            return [acc[:, slot * 128 : (slot + 1) * 128] for slot in range(4)]
+
+        def project_by_g(third, s):
+            accs = []
+            for slot in range(4):
+                acc1 = ps_m.tile([P, 512], F32, name="acc1", tag="mm")
+                accs.append(acc1[:, 0:128])
+            for g in range(4):
+                for slot in range(4):
+                    one_pass(accs[slot], third, s, slot, g)
+            return accs
 
         for s in range(4):
             acc_k = project(1, s)
@@ -183,7 +198,7 @@ def tile_attentionconv_w_kernel(tc, x, W_qkv_words, W_qkv_scales, b_qkv, out):
             for slot in range(4):
                 c = 4 * s + slot
                 nc.scalar.activation(
-                    out=k1[:, slot * 128 : (slot + 1) * 128], in_=acc_k[:, slot * 128 : (slot + 1) * 128],
+                    out=k1[:, slot * 128 : (slot + 1) * 128], in_=acc_k[slot],
                     func=ACT.Identity, bias=bias_t[:, 16 + c : 17 + c], scale=1.0,
                 )
             acc_v = project(2, s)
@@ -191,7 +206,7 @@ def tile_attentionconv_w_kernel(tc, x, W_qkv_words, W_qkv_scales, b_qkv, out):
                 c = 4 * s + slot
                 nc.vector.scalar_tensor_tensor(
                     out=kv[:, c % 2, c // 2, :, 4:12],
-                    in0=acc_v[:, slot * 128 : (slot + 1) * 128].rearrange("p (a i) -> p a i", i=8),
+                    in0=acc_v[slot].rearrange("p (a i) -> p a i", i=8),
                     scalar=bias_t[:, 32 + c : 33 + c],
                     in1=k1[:, slot * 128 : (slot + 1) * 128].rearrange("p (a i) -> p a i", i=8),
                     op0=ALU.add, op1=ALU.mult,
@@ -220,13 +235,13 @@ def tile_attentionconv_w_kernel(tc, x, W_qkv_words, W_qkv_scales, b_qkv, out):
                 )
 
         for s in range(4):
-            acc_q = project(0, s)
+            acc_q = project(0, s) if s < 3 else project_by_g(0, s)
             for slot in range(4):
                 c = 4 * s + slot
                 ch, rh = c // 2, c % 2
                 nc.vector.scalar_tensor_tensor(
                     out=oo[:, ch // 4, :, :, rh, ch % 4, :].rearrange("p j b i -> p (j b) i"),
-                    in0=acc_q[:, slot * 128 : (slot + 1) * 128].rearrange("p (a i) -> p a i", i=8),
+                    in0=acc_q[slot].rearrange("p (a i) -> p a i", i=8),
                     scalar=bias_t[:, c : c + 1],
                     in1=uu[:, rh, ch],
                     op0=ALU.add, op1=ALU.mult,

@@ -41,7 +41,7 @@ def tile_attentionconv_w_kernel(tc, x, W_qkv_words, W_qkv_scales, b_qkv, out):
 
         w_view = W_qkv_words.rearrange("g p n t -> p g (n t)")
         loads = [
-            (1, 0, 1024, 1), (2, 0, 1024, 1), (1, 1024, 1024, 1), (2, 1024, 1024, 1),
+            (1, 0, 1024, 1), (2, 0, 1024, 1), (1, 1024, 1024, 1), (2, 1024, 512, 1), (2, 1536, 512, 1),
             (0, 0, 1024, 1), (0, 1024, 512, 1), (0, 1536, 512, 4),
         ]
         w_tiles = {}

@@ -33,11 +33,6 @@ def tile_attentionconv_w_kernel(tc, x, W_qkv_words, W_qkv_scales, b_qkv, out):
 
         planes = const.tile([P, 6144], U8, name="planes", align_bytes=64)
         nc.vector.memset(planes[:].bitcast(I32), 0)
-        for quad in range(4):
-            nc.sync.dma_start(
-                out=planes[32 * quad : 32 * quad + 16, :].bitcast(I32),
-                in_=W_qkv_scales[:, 4 * quad : 4 * quad + 4, :].bitcast(I32),
-            )
 
         w_view = W_qkv_words.rearrange("g p n t -> p g (n t)")
         loads = [
@@ -62,6 +57,11 @@ def tile_attentionconv_w_kernel(tc, x, W_qkv_words, W_qkv_scales, b_qkv, out):
 
         pidx = const.tile([P, 1], I32, name="pidx")
         nc.gpsimd.iota(pidx[:], pattern=[[1, 1]], base=0, channel_multiplier=1)
+        for quad in range(4):
+            nc.gpsimd.dma_start(
+                out=planes[32 * quad : 32 * quad + 16, :].bitcast(F32),
+                in_=W_qkv_scales[:, 4 * quad : 4 * quad + 4, :].bitcast(F32),
+            )
 
         xw = xh[:].bitcast(F32).rearrange(
             "p (bg chl) (j sq u) -> p chl sq bg j u", chl=2, sq=4, u=2

@@ -36,7 +36,8 @@ def tile_attentionconv_w_kernel(tc, x, W_qkv_words, W_qkv_scales, b_qkv, out):
 
         w_view = W_qkv_words.rearrange("g p n t -> p g (n t)")
         loads = [
-            (1, 0, 1024, 1), (2, 0, 1024, 1), (1, 1024, 1024, 1), (2, 1024, 512, 1), (2, 1536, 512, 1),
+            (1, 0, 512, 1), (2, 0, 512, 1), (1, 512, 512, 1), (2, 512, 512, 1),
+            (1, 1024, 1024, 1), (2, 1024, 512, 1), (2, 1536, 512, 1),
             (0, 0, 1024, 1), (0, 1024, 512, 1), (0, 1536, 512, 4),
         ]
         w_tiles = {}
@@ -62,53 +63,6 @@ def tile_attentionconv_w_kernel(tc, x, W_qkv_words, W_qkv_scales, b_qkv, out):
                 out=planes[32 * quad : 32 * quad + 16, :].bitcast(F32),
                 in_=W_qkv_scales[:, 4 * quad : 4 * quad + 4, :].bitcast(F32),
             )
-
-        xw = xh[:].bitcast(F32).rearrange(
-            "p (bg chl) (j sq u) -> p chl sq bg j u", chl=2, sq=4, u=2
-        )
-        p1 = const.tile([P, 8, 128], F32, name="p1")
-        nc.vector.tensor_copy(
-            out=p1[:, 0:4, :].rearrange("p sq (bg j u) -> p sq bg j u", j=8, u=2),
-            in_=xw[:, 0],
-        )
-        for sq in range(4):
-            nc.scalar.copy(
-                out=p1[:, 4 + sq, :].rearrange("p (bg j u) -> p bg j u", j=8, u=2),
-                in_=xw[:, 1, sq],
-            )
-        s1 = const.tile([P, 8, 128], F32, name="s1")
-        s1v = s1[:].rearrange("p i (chl r sq) -> p chl i r sq", chl=2, sq=4)
-        for chl in range(2):
-            ps1 = ps_t.tile([P, 512], F32, name="ps1", tag="tp")
-            for sq in range(4):
-                nc.tensor.transpose(
-                    out=ps1[:, sq * 128 : (sq + 1) * 128], in_=p1[:, chl * 4 + sq, :], identity=ident[:]
-                )
-            src = ps1[:].rearrange("p (sq i r) -> p i r sq", sq=4, i=8)
-            if chl == 0:
-                nc.vector.tensor_copy(out=s1v[:, chl], in_=src)
-            else:
-                nc.scalar.copy(out=s1v[:, chl], in_=src)
-
-        fin = const.tile([P, 2048], BF16, name="fin", align_bytes=64)
-        finw = fin[:].bitcast(F32).rearrange("p (gj b i u) -> p b gj i u", gj=32, b=2, i=8, u=2)
-        for h in range(2):
-            ps2 = ps_t.tile([P, 512], F32, name="ps2", tag="tp")
-            for ii in range(4):
-                nc.tensor.transpose(
-                    out=ps2[:, ii * 128 : (ii + 1) * 128], in_=s1[:, 4 * h + ii, :], identity=ident[:]
-                )
-            src = ps2[:].rearrange("p (i b gj u) -> p b gj i u", i=4, b=2, gj=32, u=2)
-            for b in range(2):
-                dst = finw[:, b, :, 4 * h : 4 * h + 4, :]
-                if h == 0:
-                    nc.vector.tensor_copy(out=dst, in_=src[:, b])
-                else:
-                    nc.scalar.copy(out=dst, in_=src[:, b])
-
-        fcodes = const.tile([P, 512], U32, name="fcodes", align_bytes=64)
-        fsc = const.tile([P, 512], U8, name="fsc", align_bytes=64)
-        nc.vector.quantize_mx(out=fcodes[:].bitcast(FP8X4), scales=fsc[:], in_=fin[:])
 
         bz = const.tile([P, P], F32, name="bz")
         nc.vector.memset(bz[:], 0.0)
@@ -161,6 +115,53 @@ def tile_attentionconv_w_kernel(tc, x, W_qkv_words, W_qkv_scales, b_qkv, out):
         uu = const.tile([P, 2, 8, 16, 8], F32, name="uu")
         oo = const.tile([P, 2, 8, 2, 2, 4, 8], F32, name="oo")
 
+        xw = xh[:].bitcast(F32).rearrange(
+            "p (bg chl) (j sq u) -> p chl sq bg j u", chl=2, sq=4, u=2
+        )
+        p1 = const.tile([P, 8, 128], F32, name="p1")
+        nc.vector.tensor_copy(
+            out=p1[:, 0:4, :].rearrange("p sq (bg j u) -> p sq bg j u", j=8, u=2),
+            in_=xw[:, 0],
+        )
+        for sq in range(4):
+            nc.scalar.copy(
+                out=p1[:, 4 + sq, :].rearrange("p (bg j u) -> p bg j u", j=8, u=2),
+                in_=xw[:, 1, sq],
+            )
+        s1 = const.tile([P, 8, 128], F32, name="s1")
+        s1v = s1[:].rearrange("p i (chl r sq) -> p chl i r sq", chl=2, sq=4)
+        for chl in range(2):
+            ps1 = ps_t.tile([P, 512], F32, name="ps1", tag="tp")
+            for sq in range(4):
+                nc.tensor.transpose(
+                    out=ps1[:, sq * 128 : (sq + 1) * 128], in_=p1[:, chl * 4 + sq, :], identity=ident[:]
+                )
+            src = ps1[:].rearrange("p (sq i r) -> p i r sq", sq=4, i=8)
+            if chl == 0:
+                nc.vector.tensor_copy(out=s1v[:, chl], in_=src)
+            else:
+                nc.scalar.copy(out=s1v[:, chl], in_=src)
+
+        fin = const.tile([P, 2048], BF16, name="fin", align_bytes=64)
+        finw = fin[:].bitcast(F32).rearrange("p (gj b i u) -> p b gj i u", gj=32, b=2, i=8, u=2)
+        for h in range(2):
+            ps2 = ps_t.tile([P, 512], F32, name="ps2", tag="tp")
+            for ii in range(4):
+                nc.tensor.transpose(
+                    out=ps2[:, ii * 128 : (ii + 1) * 128], in_=s1[:, 4 * h + ii, :], identity=ident[:]
+                )
+            src = ps2[:].rearrange("p (i b gj u) -> p b gj i u", i=4, b=2, gj=32, u=2)
+            for b in range(2):
+                dst = finw[:, b, :, 4 * h : 4 * h + 4, :]
+                if h == 0:
+                    nc.vector.tensor_copy(out=dst, in_=src[:, b])
+                else:
+                    nc.scalar.copy(out=dst, in_=src[:, b])
+
+        fcodes = const.tile([P, 512], U32, name="fcodes", align_bytes=64)
+        fsc = const.tile([P, 512], U8, name="fsc", align_bytes=64)
+        nc.vector.quantize_mx(out=fcodes[:].bitcast(FP8X4), scales=fsc[:], in_=fin[:])
+
         def one_pass(dst, third, s, slot, g):
             wt, off = w_tiles[(third, s)]
             lc = off + slot * 128
@@ -192,7 +193,7 @@ def tile_attentionconv_w_kernel(tc, x, W_qkv_words, W_qkv_scales, b_qkv, out):
                     one_pass(accs[slot], third, s, slot, g)
             return accs
 
-        for s in range(4):
+        def k_bank(s):
             acc_k = project(1, s)
             k1 = work.tile([P, 512], F32, name="k1")
             for slot in range(4):
@@ -201,6 +202,9 @@ def tile_attentionconv_w_kernel(tc, x, W_qkv_words, W_qkv_scales, b_qkv, out):
                     out=k1[:, slot * 128 : (slot + 1) * 128], in_=acc_k[slot],
                     func=ACT.Identity, bias=bias_t[:, 16 + c : 17 + c], scale=1.0,
                 )
+            return k1
+
+        def v_bank(s, k1):
             acc_v = project(2, s)
             for slot in range(4):
                 c = 4 * s + slot
@@ -212,27 +216,41 @@ def tile_attentionconv_w_kernel(tc, x, W_qkv_words, W_qkv_scales, b_qkv, out):
                     op0=ALU.add, op1=ALU.mult,
                 )
             ch0 = 2 * s
+            kvv = [kv[:, rh, ch0 : ch0 + 2] for rh in range(2)]
+            ttv = [tt[:, rh, ch0 : ch0 + 2] for rh in range(2)]
+            tmps = []
             for rh in range(2):
-                kvv = kv[:, rh, ch0 : ch0 + 2]
                 tmp = work.tile([P, 2, 16, 8], F32, name="tmp")
+                tmps.append(tmp)
                 nc.vector.scalar_tensor_tensor(
-                    out=tmp[:], in0=kvv[:, :, :, 3:11], scalar=tab[:, 2 + rh : 3 + rh], in1=kvv[:, :, :, 4:12],
-                    op0=ALU.mult, op1=ALU.add,
+                    out=tmp[:], in0=kvv[rh][:, :, :, 3:11], scalar=tab[:, 2 + rh : 3 + rh],
+                    in1=kvv[rh][:, :, :, 4:12], op0=ALU.mult, op1=ALU.add,
                 )
-                ttv = tt[:, rh, ch0 : ch0 + 2]
+            for rh in range(2):
                 nc.vector.scalar_tensor_tensor(
-                    out=ttv[:, :, 2:18, :], in0=kvv[:, :, :, 5:13], scalar=tab[:, 4 + rh : 5 + rh], in1=tmp[:],
-                    op0=ALU.mult, op1=ALU.add,
+                    out=ttv[rh][:, :, 2:18, :], in0=kvv[rh][:, :, :, 5:13], scalar=tab[:, 4 + rh : 5 + rh],
+                    in1=tmps[rh][:], op0=ALU.mult, op1=ALU.add,
                 )
+            tmps2 = []
+            for rh in range(2):
                 tmp2 = work.tile([P, 2, 16, 8], F32, name="tmp2")
+                tmps2.append(tmp2)
                 nc.vector.scalar_tensor_tensor(
-                    out=tmp2[:], in0=ttv[:, :, 0:16, :], scalar=tab[:, 0:1], in1=ttv[:, :, 2:18, :],
-                    op0=ALU.mult, op1=ALU.add,
+                    out=tmp2[:], in0=ttv[rh][:, :, 0:16, :], scalar=tab[:, 0:1],
+                    in1=ttv[rh][:, :, 2:18, :], op0=ALU.mult, op1=ALU.add,
                 )
+            for rh in range(2):
                 nc.vector.scalar_tensor_tensor(
-                    out=uu[:, rh, ch0 : ch0 + 2], in0=ttv[:, :, 4:20, :], scalar=tab[:, 1:2], in1=tmp2[:],
-                    op0=ALU.mult, op1=ALU.add,
+                    out=uu[:, rh, ch0 : ch0 + 2], in0=ttv[rh][:, :, 4:20, :], scalar=tab[:, 1:2],
+                    in1=tmps2[rh][:], op0=ALU.mult, op1=ALU.add,
                 )
+
+        v_bank(0, k_bank(0))
+        v_bank(1, k_bank(1))
+        k1_a = k_bank(2)
+        k1_b = k_bank(3)
+        v_bank(2, k1_a)
+        v_bank(3, k1_b)
 
         for s in range(4):
             acc_q = project(0, s) if s < 3 else project_by_g(0, s)
@@ -258,10 +276,10 @@ def tile_attentionconv_w_kernel(tc, x, W_qkv_words, W_qkv_scales, b_qkv, out):
                             identity=ident[:],
                         )
                     src = pso[:].rearrange("p (j r s) -> p r j s", j=4, r=8)
-                    if hj == 0:
-                        nc.scalar.copy(out=o_rows[:, :, 0:4, :], in_=src)
+                    if hj == 0 or cg == 0:
+                        nc.scalar.copy(out=o_rows[:, :, 4 * hj : 4 * hj + 4, :], in_=src)
                     else:
-                        nc.vector.tensor_copy(out=o_rows[:, :, 4:8, :], in_=src)
+                        nc.vector.tensor_copy(out=o_rows[:, :, 4 * hj : 4 * hj + 4, :], in_=src)
                 for b in range(2):
                     dst = out[b, 4 * cg : 4 * cg + 4].rearrange("c (i rh r) w -> rh (c i) (r w)", rh=2, r=8)
                     for rh in range(2):

@@ -36,8 +36,7 @@ def tile_attentionconv_w_kernel(tc, x, W_qkv_words, W_qkv_scales, b_qkv, out):
 
         w_view = W_qkv_words.rearrange("g p n t -> p g (n t)")
         loads = [
-            (1, 0, 512, 1), (2, 0, 512, 1), (1, 512, 512, 1), (2, 512, 512, 1),
-            (1, 1024, 1024, 1), (2, 1024, 512, 1), (2, 1536, 512, 1),
+            (1, 0, 2048, 1), (2, 0, 512, 1), (2, 512, 512, 1), (2, 1024, 1024, 1),
             (0, 0, 1024, 1), (0, 1024, 512, 1), (0, 1536, 512, 4),
         ]
         w_tiles = {}

@@ -36,19 +36,21 @@ def tile_attentionconv_w_kernel(tc, x, W_qkv_words, W_qkv_scales, b_qkv, out):
 
         w_view = W_qkv_words.rearrange("g p n t -> p g (n t)")
         loads = [
-            (1, 0, 2048, 1), (2, 0, 512, 1), (2, 512, 512, 1), (2, 1024, 1024, 1),
-            (0, 0, 1024, 1), (0, 1024, 512, 1), (0, 1536, 512, 4),
+            (1, 0, 2048, 2, 2), (2, 0, 512, 2, 2), (2, 512, 512, 2, 2), (2, 1024, 1024, 2, 2),
+            (0, 0, 1024, 1, 1), (0, 1024, 512, 1, 1), (0, 1536, 512, 4, 1),
         ]
         w_tiles = {}
-        for third, c0, cols, pieces in loads:
+        for third, c0, cols, pieces, queues in loads:
             wt = wpool.tile([P, 4, cols], U32, name="w%d_%d" % (third, c0), align_bytes=64)
             n0 = third * 2048 + c0
             gs = 4 // pieces
             for piece in range(pieces):
-                nc.sync.dma_start(
-                    out=wt[:, piece * gs : (piece + 1) * gs, :].bitcast(I32),
-                    in_=w_view[:, piece * gs : (piece + 1) * gs, 4 * n0 : 4 * (n0 + cols)].bitcast(I32),
-                )
+                dst = wt[:, piece * gs : (piece + 1) * gs, :]
+                src = w_view[:, piece * gs : (piece + 1) * gs, 4 * n0 : 4 * (n0 + cols)]
+                if piece % queues == 0:
+                    nc.sync.dma_start(out=dst.bitcast(I32), in_=src.bitcast(I32))
+                else:
+                    nc.scalar.dma_start(out=dst.bitcast(F32), in_=src.bitcast(F32))
             for s in range(c0 // 512, (c0 + cols) // 512):
                 w_tiles[(third, s)] = (wt, s * 512 - c0)
 

@@ -281,10 +281,11 @@ def tile_attentionconv_w_kernel(tc, x, W_qkv_words, W_qkv_scales, b_qkv, out):
                         nc.scalar.copy(out=o_rows[:, :, 4 * hj : 4 * hj + 4, :], in_=src)
                     else:
                         nc.vector.tensor_copy(out=o_rows[:, :, 4 * hj : 4 * hj + 4, :], in_=src)
-                for b in range(2):
-                    dst = out[b, 4 * cg : 4 * cg + 4].rearrange("c (i rh r) w -> rh (c i) (r w)", rh=2, r=8)
-                    for rh in range(2):
+                for rh in range(2):
+                    for b in range(2):
+                        dst = out[b, 4 * cg : 4 * cg + 4].rearrange("c (i rh r) w -> rh (c i) (r w)", rh=2, r=8)
                         p0 = b * 64 + rh * 32
-                        nc.sync.dma_start(
+                        queue = nc.sync if b == 0 else nc.scalar
+                        queue.dma_start(
                             out=dst[rh], in_=o_rows[p0 : p0 + 32].rearrange("p r j s -> p (r j s)")
                         )

@@ -268,24 +268,24 @@ def tile_attentionconv_w_kernel(tc, x, W_qkv_words, W_qkv_scales, b_qkv, out):
             if s % 2 == 1:
                 cg = s // 2
                 o_rows = work.tile([P, 8, 8, 16], F32, name="o_rows", bufs=2)
-                for hj in range(2):
+                for part, (j0, j1) in enumerate(((0, 3), (3, 6), (6, 8))):
                     pso = ps_t.tile([P, 512], F32, name="pso", tag="tp")
-                    for jj in range(4):
+                    for j in range(j0, j1):
                         nc.tensor.transpose(
-                            out=pso[:, jj * 128 : (jj + 1) * 128],
-                            in_=oo[:, cg, 4 * hj + jj].rearrange("p b rh c i -> p (b rh c i)"),
+                            out=pso[:, (j - j0) * 128 : (j - j0 + 1) * 128],
+                            in_=oo[:, cg, j].rearrange("p b rh c i -> p (b rh c i)"),
                             identity=ident[:],
                         )
-                    src = pso[:].rearrange("p (j r s) -> p r j s", j=4, r=8)
-                    if hj == 0 or cg == 0:
-                        nc.scalar.copy(out=o_rows[:, :, 4 * hj : 4 * hj + 4, :], in_=src)
+                    src = pso[:, 0 : (j1 - j0) * 128].rearrange("p (j r s) -> p r j s", j=j1 - j0, r=8)
+                    if part != 1 or cg == 0:
+                        nc.scalar.copy(out=o_rows[:, :, j0:j1, :], in_=src)
                     else:
-                        nc.vector.tensor_copy(out=o_rows[:, :, 4 * hj : 4 * hj + 4, :], in_=src)
+                        nc.vector.tensor_copy(out=o_rows[:, :, j0:j1, :], in_=src)
                 for rh in range(2):
                     for b in range(2):
                         dst = out[b, 4 * cg : 4 * cg + 4].rearrange("c (i rh r) w -> rh (c i) (r w)", rh=2, r=8)
                         p0 = b * 64 + rh * 32
-                        queue = nc.sync if b == 0 else nc.scalar
+                        queue = nc.scalar if (b == 1 and cg == 1) else nc.sync
                         queue.dma_start(
                             out=dst[rh], in_=o_rows[p0 : p0 + 32].rearrange("p r j s -> p (r j s)")
                         )

@@ -25,8 +25,8 @@ def tile_attentionconv_w_kernel(tc, x, W_qkv_words, W_qkv_scales, b_qkv, out):
         ps_t = ctx.enter_context(tc.psum_pool(name="ps_t", bufs=3))
         ps_m = ctx.enter_context(tc.psum_pool(name="ps_m", bufs=5))
 
-        xh = const.tile([P, 16, 128], BF16, name="xh")
-        nc.sync.dma_start(out=xh[:], in_=x.rearrange("b c h w -> h (b c) w"))
+        x1 = const.tile([P, 2048], BF16, name="x1")
+        nc.sync.dma_start(out=x1[:], in_=x.rearrange("b c (i r) w -> (b c i) (r w)", r=16))
 
         bb = const.tile([48, 128], BF16, name="bb")
         nc.scalar.dma_start(out=bb[:], in_=b_qkv.rearrange("(m p) -> m p", p=128))
@@ -116,44 +116,51 @@ def tile_attentionconv_w_kernel(tc, x, W_qkv_words, W_qkv_scales, b_qkv, out):
         uu = const.tile([P, 2, 8, 16, 8], F32, name="uu")
         oo = const.tile([P, 2, 8, 2, 2, 4, 8], F32, name="oo")
 
-        xw = xh[:].bitcast(F32).rearrange(
-            "p (bg chl) (j sq u) -> p chl sq bg j u", chl=2, sq=4, u=2
-        )
-        p1 = const.tile([P, 8, 128], F32, name="p1")
-        nc.vector.tensor_copy(
-            out=p1[:, 0:4, :].rearrange("p sq (bg j u) -> p sq bg j u", j=8, u=2),
-            in_=xw[:, 0],
-        )
-        for sq in range(4):
-            nc.scalar.copy(
-                out=p1[:, 4 + sq, :].rearrange("p (bg j u) -> p bg j u", j=8, u=2),
-                in_=xw[:, 1, sq],
-            )
+        x1w = x1[:].bitcast(F32).rearrange("p (rj h sql u) -> p h u sql rj", h=2, sql=2, u=2)
+        pa = const.tile([P, 2, 2, 2, 128], F32, name="pa")
+        nc.vector.tensor_copy(out=pa[:, 0], in_=x1w[:, 0])
+        nc.scalar.copy(out=pa[:, 1], in_=x1w[:, 1])
+
+        sa = const.tile([P, 2, 4, 128], F32, name="sa")
+        for h in range(2):
+            psa = ps_t.tile([P, 512], F32, name="psa", tag="tp")
+            for slot in range(4):
+                nc.tensor.transpose(
+                    out=psa[:, slot * 128 : (slot + 1) * 128], in_=pa[:, h, slot // 2, slot % 2, :], identity=ident[:]
+                )
+            src = psa[:].rearrange("p (u sb chl i) -> p chl sb i u", u=2, sb=16, chl=2)
+            for chl in range(2):
+                dst = sa[:, chl, 2 * h : 2 * h + 2, :].rearrange("p sql (bg i u) -> p (sql bg) i u", i=8, u=2)
+                if h == 0:
+                    nc.vector.tensor_copy(out=dst, in_=src[:, chl])
+                else:
+                    nc.scalar.copy(out=dst, in_=src[:, chl])
+
         s1 = const.tile([P, 8, 128], F32, name="s1")
-        s1v = s1[:].rearrange("p i (chl r sq) -> p chl i r sq", chl=2, sq=4)
+        s1v = s1[:].rearrange("p j (chl r sq) -> p chl j r sq", chl=2, sq=4)
         for chl in range(2):
             ps1 = ps_t.tile([P, 512], F32, name="ps1", tag="tp")
             for sq in range(4):
                 nc.tensor.transpose(
-                    out=ps1[:, sq * 128 : (sq + 1) * 128], in_=p1[:, chl * 4 + sq, :], identity=ident[:]
+                    out=ps1[:, sq * 128 : (sq + 1) * 128], in_=sa[:, chl, sq, :], identity=ident[:]
                 )
-            src = ps1[:].rearrange("p (sq i r) -> p i r sq", sq=4, i=8)
+            src = ps1[:].rearrange("p (sq r j) -> p j r sq", sq=4, r=16)
             if chl == 0:
                 nc.vector.tensor_copy(out=s1v[:, chl], in_=src)
             else:
                 nc.scalar.copy(out=s1v[:, chl], in_=src)
 
         fin = const.tile([P, 2048], BF16, name="fin", align_bytes=64)
-        finw = fin[:].bitcast(F32).rearrange("p (gj b i u) -> p b gj i u", gj=32, b=2, i=8, u=2)
+        finw = fin[:].bitcast(F32).rearrange("p (g j b iu) -> p b j g iu", g=4, j=8, b=2)
         for h in range(2):
             ps2 = ps_t.tile([P, 512], F32, name="ps2", tag="tp")
-            for ii in range(4):
+            for jj in range(4):
                 nc.tensor.transpose(
-                    out=ps2[:, ii * 128 : (ii + 1) * 128], in_=s1[:, 4 * h + ii, :], identity=ident[:]
+                    out=ps2[:, jj * 128 : (jj + 1) * 128], in_=s1[:, 4 * h + jj, :], identity=ident[:]
                 )
-            src = ps2[:].rearrange("p (i b gj u) -> p b gj i u", i=4, b=2, gj=32, u=2)
+            src = ps2[:].rearrange("p (j b g iu) -> p b j g iu", j=4, b=2, g=4)
             for b in range(2):
-                dst = finw[:, b, :, 4 * h : 4 * h + 4, :]
+                dst = finw[:, b, 4 * h : 4 * h + 4]
                 if h == 0:
                     nc.vector.tensor_copy(out=dst, in_=src[:, b])
                 else:

@@ -36,8 +36,9 @@ def tile_attentionconv_w_kernel(tc, x, W_qkv_words, W_qkv_scales, b_qkv, out):
 
         w_view = W_qkv_words.rearrange("g p n t -> p g (n t)")
         loads = [
-            (1, 0, 2048, 2, 2), (2, 0, 512, 2, 2), (2, 512, 512, 2, 2), (2, 1024, 1024, 2, 2),
-            (0, 0, 1024, 1, 1), (0, 1024, 512, 1, 1), (0, 1536, 512, 4, 1),
+            (1, 0, 1024, 1, 1), (2, 0, 512, 1, 1), (2, 512, 512, 1, 1),
+            (1, 1024, 1024, 1, 1), (2, 1024, 512, 1, 1), (2, 1536, 512, 1, 1),
+            (0, 0, 512, 1, 1), (0, 512, 512, 1, 1), (0, 1024, 512, 1, 1), (0, 1536, 512, 4, 1),
         ]
         w_tiles = {}
         for third, c0, cols, pieces, queues in loads:

@@ -38,20 +38,23 @@ def tile_attentionconv_w_kernel(tc, x, W_qkv_words, W_qkv_scales, b_qkv, out):
         loads = [
             (1, 0, 1024, 1, 1), (2, 0, 512, 1, 1), (2, 512, 512, 1, 1),
             (1, 1024, 1024, 1, 1), (2, 1024, 512, 1, 1), (2, 1536, 512, 1, 1),
-            (0, 0, 512, 1, 1), (0, 512, 512, 1, 1), (0, 1024, 512, 1, 1), (0, 1536, 512, 4, 1),
+            (0, 0, 512, 1, 1), (0, 512, 512, 1, 1), (0, 1024, 512, 1, 1), (0, 1536, 512, 4, 2),
         ]
         w_tiles = {}
-        for third, c0, cols, pieces, queues in loads:
+        for third, c0, cols, pieces, last_cut in loads:
             wt = wpool.tile([P, 4, cols], U32, name="w%d_%d" % (third, c0), align_bytes=64)
             n0 = third * 2048 + c0
             gs = 4 // pieces
             for piece in range(pieces):
-                dst = wt[:, piece * gs : (piece + 1) * gs, :]
-                src = w_view[:, piece * gs : (piece + 1) * gs, 4 * n0 : 4 * (n0 + cols)]
-                if piece % queues == 0:
-                    nc.sync.dma_start(out=dst.bitcast(I32), in_=src.bitcast(I32))
-                else:
-                    nc.scalar.dma_start(out=dst.bitcast(F32), in_=src.bitcast(F32))
+                cut = last_cut if piece == pieces - 1 else 1
+                width = cols // cut
+                for part in range(cut):
+                    nc.sync.dma_start(
+                        out=wt[:, piece * gs : (piece + 1) * gs, part * width : (part + 1) * width].bitcast(I32),
+                        in_=w_view[
+                            :, piece * gs : (piece + 1) * gs, 4 * (n0 + part * width) : 4 * (n0 + (part + 1) * width)
+                        ].bitcast(I32),
+                    )
             for s in range(c0 // 512, (c0 + cols) // 512):
                 w_tiles[(third, s)] = (wt, s * 512 - c0)
 
@@ -60,7 +63,7 @@ def tile_attentionconv_w_kernel(tc, x, W_qkv_words, W_qkv_scales, b_qkv, out):
 
         pidx = const.tile([P, 1], I32, name="pidx")
         nc.gpsimd.iota(pidx[:], pattern=[[1, 1]], base=0, channel_multiplier=1)
-        for quad in range(4):
+        for quad in (0, 2, 1, 3):
             nc.gpsimd.dma_start(
                 out=planes[32 * quad : 32 * quad + 16, :].bitcast(F32),
                 in_=W_qkv_scales[:, 4 * quad : 4 * quad + 4, :].bitcast(F32),

@@ -264,7 +264,7 @@ def tile_attentionconv_w_kernel(tc, x, W_qkv_words, W_qkv_scales, b_qkv, out):
         v_bank(2, k1_a)
         v_bank(3, k1_b)
 
-        for s in range(4):
+        def q_bank(s):
             acc_q = project(0, s) if s < 3 else project_by_g(0, s)
             for slot in range(4):
                 c = 4 * s + slot
@@ -276,27 +276,35 @@ def tile_attentionconv_w_kernel(tc, x, W_qkv_words, W_qkv_scales, b_qkv, out):
                     in1=uu[:, rh, ch],
                     op0=ALU.add, op1=ALU.mult,
                 )
-            if s % 2 == 1:
-                cg = s // 2
-                o_rows = work.tile([P, 8, 8, 16], F32, name="o_rows", bufs=2)
-                for part, (j0, j1) in enumerate(((0, 3), (3, 6), (6, 8))):
-                    pso = ps_t.tile([P, 512], F32, name="pso", tag="tp")
-                    for j in range(j0, j1):
-                        nc.tensor.transpose(
-                            out=pso[:, (j - j0) * 128 : (j - j0 + 1) * 128],
-                            in_=oo[:, cg, j].rearrange("p b rh c i -> p (b rh c i)"),
-                            identity=ident[:],
-                        )
-                    src = pso[:, 0 : (j1 - j0) * 128].rearrange("p (j r s) -> p r j s", j=j1 - j0, r=8)
-                    if part != 1 or cg == 0:
-                        nc.scalar.copy(out=o_rows[:, :, j0:j1, :], in_=src)
-                    else:
-                        nc.vector.tensor_copy(out=o_rows[:, :, j0:j1, :], in_=src)
-                for rh in range(2):
-                    for b in range(2):
-                        dst = out[b, 4 * cg : 4 * cg + 4].rearrange("c (i rh r) w -> rh (c i) (r w)", rh=2, r=8)
-                        p0 = b * 64 + rh * 32
-                        queue = nc.scalar if (b == 1 and cg == 1) else nc.sync
-                        queue.dma_start(
-                            out=dst[rh], in_=o_rows[p0 : p0 + 32].rearrange("p r j s -> p (r j s)")
-                        )
+
+        def put_out(cg):
+            o_rows = work.tile([P, 8, 8, 16], F32, name="o_rows", bufs=2)
+            for part, (j0, j1) in enumerate(((0, 3), (3, 6), (6, 8))):
+                pso = ps_t.tile([P, 512], F32, name="pso", tag="tp")
+                for j in range(j0, j1):
+                    nc.tensor.transpose(
+                        out=pso[:, (j - j0) * 128 : (j - j0 + 1) * 128],
+                        in_=oo[:, cg, j].rearrange("p b rh c i -> p (b rh c i)"),
+                        identity=ident[:],
+                    )
+                src = pso[:, 0 : (j1 - j0) * 128].rearrange("p (j r s) -> p r j s", j=j1 - j0, r=8)
+                if part != 1 or cg == 0:
+                    nc.scalar.copy(out=o_rows[:, :, j0:j1, :], in_=src)
+                else:
+                    nc.vector.tensor_copy(out=o_rows[:, :, j0:j1, :], in_=src)
+            for rh in range(2):
+                for b in range(2):
+                    dst = out[b, 4 * cg : 4 * cg + 4].rearrange("c (i rh r) w -> rh (c i) (r w)", rh=2, r=8)
+                    p0 = b * 64 + rh * 32
+                    queue = nc.scalar if (b == 1 and cg == 1) else nc.sync
+                    queue.dma_start(
+                        out=dst[rh], in_=o_rows[p0 : p0 + 32].rearrange("p r j s -> p (r j s)")
+                    )
+
+        with tc.manual_schedule(engines={mybir.EngineType.PE}):
+            q_bank(0)
+            q_bank(1)
+            put_out(0)
+            q_bank(2)
+            q_bank(3)
+            put_out(1)

@@ -257,13 +257,6 @@ def tile_attentionconv_w_kernel(tc, x, W_qkv_words, W_qkv_scales, b_qkv, out):
                     in1=tmps2[rh][:], op0=ALU.mult, op1=ALU.add,
                 )
 
-        v_bank(0, k_bank(0))
-        v_bank(1, k_bank(1))
-        k1_a = k_bank(2)
-        k1_b = k_bank(3)
-        v_bank(2, k1_a)
-        v_bank(3, k1_b)
-
         def q_bank(s):
             acc_q = project(0, s) if s < 3 else project_by_g(0, s)
             for slot in range(4):
@@ -301,10 +294,18 @@ def tile_attentionconv_w_kernel(tc, x, W_qkv_words, W_qkv_scales, b_qkv, out):
                         out=dst[rh], in_=o_rows[p0 : p0 + 32].rearrange("p r j s -> p (r j s)")
                     )
 
-        with tc.manual_schedule(engines={mybir.EngineType.PE}):
+        with tc.manual_schedule(engines={mybir.EngineType.PE, mybir.EngineType.DVE}):
+            k1_a = k_bank(0)
+            k1_b = k_bank(1)
+            v_bank(0, k1_a)
+            v_bank(1, k1_b)
+            k1_a = k_bank(2)
+            k1_b = k_bank(3)
+            v_bank(2, k1_a)
+            v_bank(3, k1_b)
             q_bank(0)
             q_bank(1)
-            put_out(0)
             q_bank(2)
+            put_out(0)
             q_bank(3)
             put_out(1)

from contextlib import ExitStack

import concourse.mybir as mybir
from concourse.masks import make_identity

F32 = mybir.dt.float32
BF16 = mybir.dt.bfloat16
I32 = mybir.dt.int32
U32 = mybir.dt.uint32
U8 = mybir.dt.uint8
FP8X4 = mybir.dt.float8_e4m3fn_x4
ALU = mybir.AluOpType
ACT = mybir.ActivationFunctionType

P = 128
FLOPS = 2 * 128 * 2048 * 6144


def tile_attentionconv_w_kernel(tc, x, W_qkv_words, W_qkv_scales, b_qkv, out):
    nc = tc.nc
    with ExitStack() as ctx:
        const = ctx.enter_context(tc.tile_pool(name="const", bufs=1))
        wpool = ctx.enter_context(tc.tile_pool(name="wpool", bufs=1))
        work = ctx.enter_context(tc.tile_pool(name="work", bufs=3))
        ps_t = ctx.enter_context(tc.psum_pool(name="ps_t", bufs=3))
        ps_m = ctx.enter_context(tc.psum_pool(name="ps_m", bufs=5))

        x1 = const.tile([P, 2048], BF16, name="x1")
        nc.sync.dma_start(out=x1[:], in_=x.rearrange("b c (i r) w -> (b c i) (r w)", r=16))

        bb = const.tile([48, 128], BF16, name="bb")
        nc.scalar.dma_start(out=bb[:], in_=b_qkv.rearrange("(m p) -> m p", p=128))

        planes = const.tile([P, 6144], U8, name="planes", align_bytes=64)
        nc.vector.memset(planes[:].bitcast(I32), 0)

        w_view = W_qkv_words.rearrange("g p n t -> p g (n t)")
        loads = [
            (1, 0, 1024, 1, 1), (2, 0, 512, 1, 1), (2, 512, 512, 1, 1),
            (1, 1024, 1024, 1, 1), (2, 1024, 512, 1, 1), (2, 1536, 512, 1, 1),
            (0, 0, 512, 1, 1), (0, 512, 512, 1, 1), (0, 1024, 512, 1, 1), (0, 1536, 512, 4, 2),
        ]
        w_tiles = {}
        for third, c0, cols, pieces, last_cut in loads:
            wt = wpool.tile([P, 4, cols], U32, name="w%d_%d" % (third, c0), align_bytes=64)
            n0 = third * 2048 + c0
            gs = 4 // pieces
            for piece in range(pieces):
                cut = last_cut if piece == pieces - 1 else 1
                width = cols // cut
                for part in range(cut):
                    nc.sync.dma_start(
                        out=wt[:, piece * gs : (piece + 1) * gs, part * width : (part + 1) * width].bitcast(I32),
                        in_=w_view[
                            :, piece * gs : (piece + 1) * gs, 4 * (n0 + part * width) : 4 * (n0 + (part + 1) * width)
                        ].bitcast(I32),
                    )
            for s in range(c0 // 512, (c0 + cols) // 512):
                w_tiles[(third, s)] = (wt, s * 512 - c0)

        ident = const.tile([P, P], F32, name="ident")
        make_identity(nc, ident[:])

        pidx = const.tile([P, 1], I32, name="pidx")
        nc.gpsimd.iota(pidx[:], pattern=[[1, 1]], base=0, channel_multiplier=1)
        for quad in (0, 2, 1, 3):
            nc.gpsimd.dma_start(
                out=planes[32 * quad : 32 * quad + 16, :].bitcast(F32),
                in_=W_qkv_scales[:, 4 * quad : 4 * quad + 4, :].bitcast(F32),
            )

        bz = const.tile([P, P], F32, name="bz")
        nc.vector.memset(bz[:], 0.0)
        nc.vector.tensor_copy(out=bz[0:48, :], in_=bb[:])
        psb = ps_t.tile([P, 512], F32, name="psb", tag="tp")
        nc.tensor.transpose(out=psb[:, 0:128], in_=bz[:], identity=ident[:])
        bias_t = const.tile([P, 48], F32, name="bias_t")
        nc.vector.tensor_copy(out=bias_t[:], in_=psb[:, 0:48])

        si = const.tile([P, 2], I32, name="si")
        nc.vector.tensor_single_scalar(out=si[:, 0:1], in_=pidx[:], scalar=15, op=ALU.bitwise_and)
        nc.vector.tensor_single_scalar(out=si[:, 1:2], in_=pidx[:], scalar=4, op=ALU.arith_shift_right)
        sf = const.tile([P, 2], F32, name="sf")
        nc.vector.tensor_copy(out=sf[:], in_=si[:])
        arg = const.tile([P, 6], F32, name="arg")
        specs = [(0, -15.0, 0.125), (0, 0.0, -0.125), (1, -15.0, 0.125), (1, -7.0, 0.125), (1, 0.0, -0.125), (1, 8.0, -0.125)]
        for col, (which, shift, factor) in enumerate(specs):
            nc.vector.tensor_scalar(
                out=arg[:, col : col + 1], in0=sf[:, which : which + 1],
                scalar1=shift, scalar2=factor, op0=ALU.add, op1=ALU.mult,
            )
        tab = const.tile([P, 6], F32, name="tab")
        nc.scalar.activation(out=tab[:], in_=arg[:], func=ACT.Exp)
        sar = const.tile([P, 2], F32, name="sar")
        nc.vector.tensor_tensor(out=sar[:], in0=tab[:, 2:4], in1=tab[:, 4:6], op=ALU.add)
        nc.vector.tensor_single_scalar(out=sar[:], in_=sar[:], scalar=1.0, op=ALU.add)

        beta = const.tile([P, 2, 8], F32, name="beta")
        nc.vector.tensor_tensor(
            out=beta[:],
            in0=bias_t[:, 16:32].rearrange("p (ch rh) -> p rh ch", rh=2),
            in1=bias_t[:, 32:48].rearrange("p (ch rh) -> p rh ch", rh=2),
            op=ALU.mult,
        )
        betar = const.tile([P, 2, 8], F32, name="betar")
        nc.vector.tensor_tensor(
            out=betar[:], in0=beta[:], in1=sar[:].unsqueeze(2).to_broadcast([P, 2, 8]), op=ALU.mult
        )

        kv = const.tile([P, 2, 8, 16, 16], F32, name="kv")
        nc.vector.tensor_copy(
            out=kv[:, :, :, :, 3:13:9],
            in_=beta[:].unsqueeze(3).unsqueeze(4).to_broadcast([P, 2, 8, 16, 2]),
        )
        tt = const.tile([P, 2, 8, 20, 8], F32, name="tt")
        nc.vector.tensor_copy(
            out=tt[:].rearrange("p a c (j q) i -> p a c j (q i)", q=2)[:, :, :, 0:10:9, :],
            in_=betar[:].unsqueeze(3).unsqueeze(4).to_broadcast([P, 2, 8, 2, 16]),
        )
        uu = const.tile([P, 2, 8, 16, 8], F32, name="uu")
        oo = const.tile([P, 2, 8, 2, 2, 4, 8], F32, name="oo")

        x1w = x1[:].bitcast(F32).rearrange("p (rj h sql u) -> p h u sql rj", h=2, sql=2, u=2)
        pa = const.tile([P, 2, 2, 2, 128], F32, name="pa")
        nc.vector.tensor_copy(out=pa[:, 0], in_=x1w[:, 0])
        nc.scalar.copy(out=pa[:, 1], in_=x1w[:, 1])

        sa = const.tile([P, 2, 4, 128], F32, name="sa")
        for h in range(2):
            psa = ps_t.tile([P, 512], F32, name="psa", tag="tp")
            for slot in range(4):
                nc.tensor.transpose(
                    out=psa[:, slot * 128 : (slot + 1) * 128], in_=pa[:, h, slot // 2, slot % 2, :], identity=ident[:]
                )
            src = psa[:].rearrange("p (u sb chl i) -> p chl sb i u", u=2, sb=16, chl=2)
            for chl in range(2):
                dst = sa[:, chl, 2 * h : 2 * h + 2, :].rearrange("p sql (bg i u) -> p (sql bg) i u", i=8, u=2)
                if h == 0:
                    nc.vector.tensor_copy(out=dst, in_=src[:, chl])
                else:
                    nc.scalar.copy(out=dst, in_=src[:, chl])

        s1 = const.tile([P, 8, 128], F32, name="s1")
        s1v = s1[:].rearrange("p j (chl r sq) -> p chl j r sq", chl=2, sq=4)
        for chl in range(2):
            ps1 = ps_t.tile([P, 512], F32, name="ps1", tag="tp")
            for sq in range(4):
                nc.tensor.transpose(
                    out=ps1[:, sq * 128 : (sq + 1) * 128], in_=sa[:, chl, sq, :], identity=ident[:]
                )
            src = ps1[:].rearrange("p (sq r j) -> p j r sq", sq=4, r=16)
            if chl == 0:
                nc.vector.tensor_copy(out=s1v[:, chl], in_=src)
            else:
                nc.scalar.copy(out=s1v[:, chl], in_=src)

        fin = const.tile([P, 2048], BF16, name="fin", align_bytes=64)
        finw = fin[:].bitcast(F32).rearrange("p (g j b iu) -> p b j g iu", g=4, j=8, b=2)
        for h in range(2):
            ps2 = ps_t.tile([P, 512], F32, name="ps2", tag="tp")
            for jj in range(4):
                nc.tensor.transpose(
                    out=ps2[:, jj * 128 : (jj + 1) * 128], in_=s1[:, 4 * h + jj, :], identity=ident[:]
                )
            src = ps2[:].rearrange("p (j b g iu) -> p b j g iu", j=4, b=2, g=4)
            for b in range(2):
                dst = finw[:, b, 4 * h : 4 * h + 4]
                if h == 0:
                    nc.vector.tensor_copy(out=dst, in_=src[:, b])
                else:
                    nc.scalar.copy(out=dst, in_=src[:, b])

        fcodes = const.tile([P, 512], U32, name="fcodes", align_bytes=64)
        fsc = const.tile([P, 512], U8, name="fsc", align_bytes=64)
        nc.vector.quantize_mx(out=fcodes[:].bitcast(FP8X4), scales=fsc[:], in_=fin[:])

        def one_pass(dst, third, s, slot, g):
            wt, off = w_tiles[(third, s)]
            lc = off + slot * 128
            n0 = third * 2048 + s * 512 + slot * 128
            nc.tensor.matmul_mx(
                out=dst,
                lhsT=wt[:, g, lc : lc + 128].bitcast(FP8X4),
                lhsT_scale=planes[4 * g : 128, n0 : n0 + 128],
                rhs=fcodes[:, g * 128 : (g + 1) * 128].bitcast(FP8X4),
                rhs_scale=fsc[:, g * 128 : (g + 1) * 128],
                start=(g == 0),
                stop=(g == 3),
            )

        def project(third, s):
            acc = ps_m.tile([P, 512], F32, name="acc", tag="mm")
            for slot in range(4):
                for g in range(4):
                    one_pass(acc[:, slot * 128 : (slot + 1) * 128], third, s, slot, g)
            return [acc[:, slot * 128 : (slot + 1) * 128] for slot in range(4)]

        def project_by_g(third, s):
            accs = []
            for slot in range(4):
                acc1 = ps_m.tile([P, 512], F32, name="acc1", tag="mm")
                accs.append(acc1[:, 0:128])
            for g in range(4):
                for slot in range(4):
                    one_pass(accs[slot], third, s, slot, g)
            return accs

        def k_bank(s):
            acc_k = project(1, s)
            k1 = work.tile([P, 512], F32, name="k1")
            for slot in range(4):
                c = 4 * s + slot
                nc.scalar.activation(
                    out=k1[:, slot * 128 : (slot + 1) * 128], in_=acc_k[slot],
                    func=ACT.Identity, bias=bias_t[:, 16 + c : 17 + c], scale=1.0,
                )
            return k1

        def v_bank(s, k1):
            acc_v = project(2, s)
            for slot in range(4):
                c = 4 * s + slot
                nc.vector.scalar_tensor_tensor(
                    out=kv[:, c % 2, c // 2, :, 4:12],
                    in0=acc_v[slot].rearrange("p (a i) -> p a i", i=8),
                    scalar=bias_t[:, 32 + c : 33 + c],
                    in1=k1[:, slot * 128 : (slot + 1) * 128].rearrange("p (a i) -> p a i", i=8),
                    op0=ALU.add, op1=ALU.mult,
                )
            ch0 = 2 * s
            kvv = [kv[:, rh, ch0 : ch0 + 2] for rh in range(2)]
            ttv = [tt[:, rh, ch0 : ch0 + 2] for rh in range(2)]
            tmps = []
            for rh in range(2):
                tmp = work.tile([P, 2, 16, 8], F32, name="tmp")
                tmps.append(tmp)
                nc.vector.scalar_tensor_tensor(
                    out=tmp[:], in0=kvv[rh][:, :, :, 3:11], scalar=tab[:, 2 + rh : 3 + rh],
                    in1=kvv[rh][:, :, :, 4:12], op0=ALU.mult, op1=ALU.add,
                )
            for rh in range(2):
                nc.vector.scalar_tensor_tensor(
                    out=ttv[rh][:, :, 2:18, :], in0=kvv[rh][:, :, :, 5:13], scalar=tab[:, 4 + rh : 5 + rh],
                    in1=tmps[rh][:], op0=ALU.mult, op1=ALU.add,
                )
            tmps2 = []
            for rh in range(2):
                tmp2 = work.tile([P, 2, 16, 8], F32, name="tmp2")
                tmps2.append(tmp2)
                nc.vector.scalar_tensor_tensor(
                    out=tmp2[:], in0=ttv[rh][:, :, 0:16, :], scalar=tab[:, 0:1],
                    in1=ttv[rh][:, :, 2:18, :], op0=ALU.mult, op1=ALU.add,
                )
            for rh in range(2):
                nc.vector.scalar_tensor_tensor(
                    out=uu[:, rh, ch0 : ch0 + 2], in0=ttv[rh][:, :, 4:20, :], scalar=tab[:, 1:2],
                    in1=tmps2[rh][:], op0=ALU.mult, op1=ALU.add,
                )

        def q_bank(s):
            acc_q = project(0, s) if s < 3 else project_by_g(0, s)
            for slot in range(4):
                c = 4 * s + slot
                ch, rh = c // 2, c % 2
                nc.vector.scalar_tensor_tensor(
                    out=oo[:, ch // 4, :, :, rh, ch % 4, :].rearrange("p j b i -> p (j b) i"),
                    in0=acc_q[slot].rearrange("p (a i) -> p a i", i=8),
                    scalar=bias_t[:, c : c + 1],
                    in1=uu[:, rh, ch],
                    op0=ALU.add, op1=ALU.mult,
                )

        def put_out(cg):
            o_rows = work.tile([P, 8, 8, 16], F32, name="o_rows", bufs=2)
            for part, (j0, j1) in enumerate(((0, 3), (3, 6), (6, 8))):
                pso = ps_t.tile([P, 512], F32, name="pso", tag="tp")
                for j in range(j0, j1):
                    nc.tensor.transpose(
                        out=pso[:, (j - j0) * 128 : (j - j0 + 1) * 128],
                        in_=oo[:, cg, j].rearrange("p b rh c i -> p (b rh c i)"),
                        identity=ident[:],
                    )
                src = pso[:, 0 : (j1 - j0) * 128].rearrange("p (j r s) -> p r j s", j=j1 - j0, r=8)
                if part != 1 or cg == 0:
                    nc.scalar.copy(out=o_rows[:, :, j0:j1, :], in_=src)
                else:
                    nc.vector.tensor_copy(out=o_rows[:, :, j0:j1, :], in_=src)
            for rh in range(2):
                for b in range(2):
                    dst = out[b, 4 * cg : 4 * cg + 4].rearrange("c (i rh r) w -> rh (c i) (r w)", rh=2, r=8)
                    p0 = b * 64 + rh * 32
                    queue = nc.scalar if (b == 1 and cg == 1) else nc.sync
                    queue.dma_start(
                        out=dst[rh], in_=o_rows[p0 : p0 + 32].rearrange("p r j s -> p (r j s)")
                    )

        with tc.manual_schedule(engines={mybir.EngineType.PE, mybir.EngineType.DVE}):
            k1_a = k_bank(0)
            k1_b = k_bank(1)
            v_bank(0, k1_a)
            v_bank(1, k1_b)
            k1_a = k_bank(2)
            k1_b = k_bank(3)
            v_bank(2, k1_a)
            v_bank(3, k1_b)
            q_bank(0)
            q_bank(1)
            q_bank(2)
            put_out(0)
            q_bank(3)
            put_out(1)
